import numpy as np
import ml_dtypes


def mxq(x, axis, fmt="e4m3"):
    dtype, down = {"e4m3": (ml_dtypes.float8_e4m3fn, 7), "e5m2": (ml_dtypes.float8_e5m2, 14)}[fmt]
    v = np.moveaxis(np.asarray(x, np.float32).astype(ml_dtypes.bfloat16).astype(np.float64), axis, -1)
    blocks = v.reshape(v.shape[:-1] + (-1, 32))
    amax = np.abs(blocks).max(-1, keepdims=True)
    byte = np.maximum(np.where(amax > 0, np.frexp(amax)[1] - 1 + 127, 0) - down, 1)
    scale = np.exp2(byte - 127.0)
    codes = (blocks / scale).astype(np.float32).astype(dtype).astype(np.float64)
    return np.moveaxis((codes * scale).reshape(v.shape), -1, axis)


WIDE = False


def mx_kscale(k):
    if not WIDE:
        return np.ones(k)
    levels = np.array([10, -10, 5, -5, 0])
    if k % 512:
        return np.exp2(np.random.permutation(np.resize(levels, k // 32))).repeat(32)
    a = np.empty((k // 512, 16))
    for p in range(k // 512):
        a[p, :8] = np.random.permutation(np.resize(levels, 8))
        for g in range(8):
            far = levels[np.abs(levels - a[p, g]) >= 10]
            a[p, g + 8] = far[np.random.randint(len(far))]
    return np.exp2(a.ravel()).repeat(32)


BF16 = ml_dtypes.bfloat16


def bf(x):
    return np.asarray(x, np.float32).astype(BF16)


def f64(x):
    return np.asarray(x).astype(np.float64)


N, H, S, R, T = 4096, 512, 4, 128, 128


def setup_inputs():
    s = mx_kscale(H)
    return {"encodings": bf(np.random.standard_normal((N, H)) * s),
            "domain_encs": bf(np.random.standard_normal((S, H)) * s),
            "Us": bf(np.random.standard_normal((S, H, R)) / np.sqrt(H) / s[None, :, None])}


def reference(encodings, domain_encs, Us):
    diff = f64(encodings)[None, :, :] - f64(domain_encs)[:, None, :]
    proj = mxq(diff, 2, "e4m3") @ mxq(f64(Us), 1, "e4m3")
    dist = np.sqrt(np.sum(proj * proj, axis=-1))
    z = -dist
    e = np.exp(z - z.max(axis=0, keepdims=True))
    return e / e.sum(axis=0, keepdims=True)

@@ -1,0 +1,243 @@
+from contextlib import ExitStack
+
+import concourse.mybir as mybir
+from concourse.masks import make_identity
+
+F32 = mybir.dt.float32
+BF16 = mybir.dt.bfloat16
+U32 = mybir.dt.uint32
+U8 = mybir.dt.uint8
+FP8X4 = mybir.dt.float8_e4m3fn_x4
+ALU = mybir.AluOpType
+ACT = mybir.ActivationFunctionType
+AX = mybir.AxisListType
+
+P = 128
+N_TOK, H, S, R = 4096, 512, 4, 128
+NT = N_TOK // P
+REP = 8
+GS = 40
+LOADS = [1, 1, 2, 4, 8, 16]
+U_AFTER = 2
+UNITS = [(0, 1), (1, 1), (2, 2)] + [(j, 2) for j in range(6, 30, 2)] + [(30, 1), (31, 1)]
+SC_UNIT = (4, 2)
+SC_FIRST = 4
+SC_PER_STEP = 2
+SC_QUANT = 12
+LAG = 3
+
+FLOPS = 2 * S * N_TOK * H * R
+
+
+def tile_moe_pa_kernel(tc, encodings, domain_encs, Us, out):
+    nc = tc.nc
+    nu = len(UNITS)
+    sc = nu
+    unit = dict(enumerate(UNITS))
+    unit[sc] = SC_UNIT
+    assert sum([c for (j, c) in UNITS]) + SC_UNIT[1] == NT and sum(LOADS) == NT
+
+    with ExitStack() as ctx:
+        keep = ctx.enter_context(tc.tile_pool(name="keep", bufs=1))
+        work = ctx.enter_context(tc.tile_pool(name="work", bufs=3))
+        mxp = ctx.enter_context(tc.tile_pool(name="mxp", bufs=4))
+        ps_t = ctx.enter_context(tc.psum_pool(name="ps_t", bufs=3))
+        ps_s = ctx.enter_context(tc.psum_pool(name="ps_s", bufs=1))
+        ps_m = ctx.enter_context(tc.psum_pool(name="ps_m", bufs=4))
+        ctx.enter_context(tc.manual_schedule())
+
+        dsrc = keep.tile([P, H], BF16)
+        nc.gpsimd.memset(dsrc[:].bitcast(F32), 0.0)
+        nc.sync.dma_start(out=dsrc[0:S, :], in_=domain_encs)
+        one = keep.tile([P, 1], F32)
+        nc.vector.memset(one[:], 1.0)
+        warm = keep.tile([P, 1], F32)
+        nc.scalar.activation(out=warm[:], in_=one[:], func=ACT.Sqrt)
+        ident = keep.tile([P, P], F32)
+        make_identity(nc, ident[:])
+
+        x_all = keep.tile([P, NT, H], BF16)
+        enc_v = encodings.rearrange("(p j) h -> p j h", j=NT)
+        uraw = keep.tile([P, S * 4 * R], BF16)
+
+        j0 = 0
+        for i, cnt in enumerate(LOADS):
+            if i == U_AFTER:
+                nc.sync.dma_start(
+                    out=uraw[:].rearrange("p (s w) -> p s w", w=4 * R),
+                    in_=Us.rearrange("s (p t) r -> p s (t r)", t=4),
+                )
+            nc.sync.dma_start(out=x_all[:, j0 : j0 + cnt, :], in_=enc_v[:, j0 : j0 + cnt, :])
+            j0 += cnt
+
+        dps = ps_t.tile([P, 2, P], F32, tag="tp")
+        for u in range(2):
+            nc.tensor.transpose(dps[:, u, :], dsrc[:].bitcast(F32)[:, u : 2 * P : 2], ident[:])
+        domrep = keep.tile([P, S, REP * 4], BF16)
+        nc.vector.tensor_copy(
+            out=domrep[:].bitcast(F32).rearrange("p s (r u) -> p s r u", u=2),
+            in_=dps[:, :, 0:S].rearrange("p u s -> p s u").unsqueeze(2).to_broadcast([P, S, REP, 2]),
+        )
+        negdom = keep.tile([P, S, 4], F32)
+
+        ugr = keep.tile([P, S * R * 4], BF16, align_bytes=64)
+        ucodes = keep.tile([P, S * R], U32, align_bytes=64)
+        uscl = keep.tile([P, S * R], U8, align_bytes=64)
+        d2 = keep.tile([P, S, NT], F32)
+        dt_sc = keep.tile([P, S, SC_UNIT[1] * P * 4], BF16, align_bytes=64)
+
+        tps = {}
+        dts = {sc: dt_sc}
+        cds = {}
+        scs = {}
+        w = REP * 4
+
+        def stage_t(b):
+            first, c = unit[b]
+            if b == sc:
+                tp = ps_s.tile([P, c * P, 2], F32, tag="ts")
+            else:
+                tp = ps_t.tile([P, c * P, 2], F32, tag="tp")
+            for i in range(c):
+                xw = x_all[:, first + i, :].bitcast(F32)
+                for u in range(2):
+                    nc.tensor.transpose(tp[:, i * P : (i + 1) * P, u], xw[:, u : 2 * P : 2], ident[:])
+            tps[b] = tp
+
+        def stage_d(b):
+            c = unit[b][1]
+            gs = GS if c == 2 else 0
+            nv = c * P - gs
+            dt = work.tile([P, S, c * P * 4], BF16, tag="dt", align_bytes=64)
+            bank = tps[b][:].rearrange("p n u -> p (n u)")
+            if gs:
+                eg = work.tile([P, gs * 4], BF16, tag="eg")
+                nc.vector.tensor_copy(out=eg[:].bitcast(F32), in_=bank[:, nv * 2 :])
+                nc.gpsimd.tensor_tensor(
+                    out=dt[:, :, nv * 4 :].rearrange("p s (g w) -> p s g w", w=w),
+                    in0=eg[:].rearrange("p (g w) -> p g w", w=w).unsqueeze(1).to_broadcast([P, S, gs // REP, w]),
+                    in1=domrep[:].unsqueeze(2).to_broadcast([P, S, gs // REP, w]),
+                    op=ALU.subtract,
+                )
+            nc.vector.tensor_tensor(
+                out=dt[:, :, 0 : nv * 4].rearrange("p s (g w) -> p s g w", w=w),
+                in0=bank[:, 0 : nv * 2]
+                .bitcast(BF16)
+                .rearrange("p (g w) -> p g w", w=w)
+                .unsqueeze(1)
+                .to_broadcast([P, S, nv // REP, w]),
+                in1=domrep[:].unsqueeze(2).to_broadcast([P, S, nv // REP, w]),
+                op=ALU.subtract,
+            )
+            dts[b] = dt
+
+        def sc_piece(i):
+            s, t = divmod(i, 4)
+            nc.scalar.activation(
+                out=dt_sc[:, s, :].rearrange("p (n t) -> p n t", t=4)[:, :, t],
+                in_=tps[sc][:].rearrange("p n u -> p (n u)").bitcast(BF16).rearrange("p (n t) -> p n t", t=4)[:, :, t],
+                func=ACT.Identity,
+                bias=negdom[:, s, t : t + 1],
+                scale=1.0,
+            )
+
+        def stage_q(b):
+            c = unit[b][1]
+            cd = mxp.tile([P, S * c * P], U32, tag="cd", align_bytes=64)
+            sl = mxp.tile([P, S * c * P], U8, tag="sl", align_bytes=64)
+            nc.vector.quantize_mx(
+                out=cd[:].bitcast(FP8X4),
+                scales=sl[:],
+                in_=dts[b][:].rearrange("p s w -> p (s w)"),
+            )
+            cds[b] = cd
+            scs[b] = sl
+
+        def stage_m(b):
+            c = unit[b][1]
+            pjs = []
+            for i in range(c):
+                pj = ps_m.tile([P, S * R], F32, tag="pj")
+                for s in range(S):
+                    col = (s * c + i) * P
+                    nc.tensor.matmul_mx(
+                        out=pj[:, s * R : (s + 1) * R],
+                        lhsT=cds[b][:, col : col + P].bitcast(FP8X4),
+                        lhsT_scale=scs[b][:, col : col + P],
+                        rhs=ucodes[:, s * R : (s + 1) * R].bitcast(FP8X4),
+                        rhs_scale=uscl[:, s * R : (s + 1) * R],
+                        start=True,
+                        stop=True,
+                    )
+                pjs.append(pj)
+            return pjs
+
+        def stage_s(b, pjs):
+            for i, pj in enumerate(pjs):
+                j = unit[b][0] + i
+                for s in range(S):
+                    junk = work.tile([P, R], BF16, tag="junk")
+                    nc.scalar.activation(
+                        out=junk[:],
+                        in_=pj[:, s * R : (s + 1) * R],
+                        func=ACT.Square,
+                        accum_out=d2[:, s, j : j + 1],
+                    )
+
+        def u_regroup(s):
+            nc.scalar.copy(
+                out=ugr[:, s * R * 4 : (s + 1) * R * 4].rearrange("p (r t) -> p r t", t=4),
+                in_=uraw[:, s * R * 4 : (s + 1) * R * 4].rearrange("p (t r) -> p r t", t=4),
+            )
+
+        for k in range(nu + LAG):
+            if k < nu:
+                stage_t(k)
+            if k == SC_FIRST - 1:
+                stage_t(sc)
+            done = []
+            if k >= LAG:
+                done.append((k - LAG, stage_m(k - LAG)))
+            if k == SC_QUANT + LAG:
+                done.append((sc, stage_m(sc)))
+            if k == 1 or k == 2:
+                u_regroup(2 * k - 2)
+                u_regroup(2 * k - 1)
+            if k < nu:
+                stage_d(k)
+            if k == 2:
+                nc.vector.quantize_mx(out=ucodes[:].bitcast(FP8X4), scales=uscl[:], in_=ugr[:])
+                nc.vector.tensor_scalar(
+                    out=negdom[:], in0=domrep[:, :, 0:4], scalar1=-1.0, scalar2=None, op0=ALU.mult
+                )
+            if 1 <= k <= nu:
+                stage_q(k - 1)
+            if k == SC_QUANT:
+                stage_q(sc)
+            for i in range(SC_PER_STEP * (k - SC_FIRST), SC_PER_STEP * (k - SC_FIRST + 1)):
+                if 0 <= i < 4 * S:
+                    sc_piece(i)
+            for b, pjs in done:
+                stage_s(b, pjs)
+
+        dist = keep.tile([P, S, NT], F32)
+        nc.scalar.activation(out=dist[:], in_=d2[:], func=ACT.Sqrt, bias=1e-30)
+        warm2 = keep.tile([P, 1], F32)
+        nc.scalar.activation(out=warm2[:], in_=dist[:, 0, 0:1], func=ACT.Exp, scale=-1.0)
+        dmin = keep.tile([P, NT], F32)
+        nc.vector.tensor_reduce(out=dmin[:], in_=dist[:].rearrange("p s j -> p j s"), axis=AX.X, op=ALU.min)
+        z = keep.tile([P, S, NT], F32)
+        nc.vector.tensor_tensor(
+            out=z[:], in0=dmin[:].unsqueeze(1).to_broadcast([P, S, NT]), in1=dist[:], op=ALU.subtract
+        )
+        e = keep.tile([P, S, NT], F32)
+        nc.scalar.activation(out=e[:], in_=z[:], func=ACT.Exp)
+        esum = keep.tile([P, NT], F32)
+        nc.vector.tensor_reduce(out=esum[:], in_=e[:].rearrange("p s j -> p j s"), axis=AX.X, op=ALU.add)
+        rsum = keep.tile([P, NT], F32)
+        nc.vector.reciprocal(out=rsum[:], in_=esum[:])
+        res = keep.tile([P, S, NT], F32)
+        nc.vector.tensor_tensor(
+            out=res[:], in0=e[:], in1=rsum[:].unsqueeze(1).to_broadcast([P, S, NT]), op=ALU.mult
+        )
+        nc.sync.dma_start(out=out.rearrange("s (p j) -> p s j", j=NT), in_=res[:])

@@ -46,9 +46,8 @@ def tile_moe_pa_kernel(tc, encodings, domain_encs, Us, out):
         ps_m = ctx.enter_context(tc.psum_pool(name="ps_m", bufs=4))
         ctx.enter_context(tc.manual_schedule())
 
-        dsrc = keep.tile([P, H], BF16)
-        nc.gpsimd.memset(dsrc[:].bitcast(F32), 0.0)
-        nc.sync.dma_start(out=dsrc[0:S, :], in_=domain_encs)
+        domq = keep.tile([P, S, 4], BF16)
+        nc.scalar.dma_start(out=domq[:], in_=domain_encs.rearrange("s (p t) -> p s t", t=4))
         one = keep.tile([P, 1], F32)
         nc.vector.memset(one[:], 1.0)
         warm = keep.tile([P, 1], F32)
@@ -70,13 +69,10 @@ def tile_moe_pa_kernel(tc, encodings, domain_encs, Us, out):
             nc.sync.dma_start(out=x_all[:, j0 : j0 + cnt, :], in_=enc_v[:, j0 : j0 + cnt, :])
             j0 += cnt
 
-        dps = ps_t.tile([P, 2, P], F32, tag="tp")
-        for u in range(2):
-            nc.tensor.transpose(dps[:, u, :], dsrc[:].bitcast(F32)[:, u : 2 * P : 2], ident[:])
         domrep = keep.tile([P, S, REP * 4], BF16)
         nc.vector.tensor_copy(
-            out=domrep[:].bitcast(F32).rearrange("p s (r u) -> p s r u", u=2),
-            in_=dps[:, :, 0:S].rearrange("p u s -> p s u").unsqueeze(2).to_broadcast([P, S, REP, 2]),
+            out=domrep[:].rearrange("p s (r t) -> p s r t", t=4),
+            in_=domq[:].unsqueeze(2).to_broadcast([P, S, REP, 4]),
         )
         negdom = keep.tile([P, S, 4], F32)
 
@@ -145,11 +141,14 @@ def tile_moe_pa_kernel(tc, encodings, domain_encs, Us, out):
             c = unit[b][1]
             cd = mxp.tile([P, S * c * P], U32, tag="cd", align_bytes=64)
             sl = mxp.tile([P, S * c * P], U8, tag="sl", align_bytes=64)
-            nc.vector.quantize_mx(
-                out=cd[:].bitcast(FP8X4),
-                scales=sl[:],
-                in_=dts[b][:].rearrange("p s w -> p (s w)"),
-            )
+            parts = 2 if b == nu - 1 else 1
+            n = S * c * P // parts
+            for h in range(parts):
+                nc.vector.quantize_mx(
+                    out=cd[:, h * n : (h + 1) * n].bitcast(FP8X4),
+                    scales=sl[:, h * n : (h + 1) * n],
+                    in_=dts[b][:].rearrange("p s w -> p (s w)")[:, h * n * 4 : (h + 1) * n * 4],
+                )
             cds[b] = cd
             scs[b] = sl
 
@@ -208,7 +207,7 @@ def tile_moe_pa_kernel(tc, encodings, domain_encs, Us, out):
             if k == 2:
                 nc.vector.quantize_mx(out=ucodes[:].bitcast(FP8X4), scales=uscl[:], in_=ugr[:])
                 nc.vector.tensor_scalar(
-                    out=negdom[:], in0=domrep[:, :, 0:4], scalar1=-1.0, scalar2=None, op0=ALU.mult
+                    out=negdom[:], in0=domq[:], scalar1=-1.0, scalar2=None, op0=ALU.mult
                 )
             if 1 <= k <= nu:
                 stage_q(k - 1)

@@ -19,12 +19,15 @@ REP = 8
 GS = 40
 LOADS = [1, 1, 2, 4, 8, 16]
 U_AFTER = 2
-UNITS = [(0, 1), (1, 1), (2, 2)] + [(j, 2) for j in range(6, 30, 2)] + [(30, 1), (31, 1)]
-SC_UNIT = (4, 2)
-SC_FIRST = 4
-SC_PER_STEP = 2
-SC_QUANT = 12
-LAG = 3
+UNITS = [(0, 1), (1, 1), (2, 2)] + [(j, 2) for j in range(8, 30, 2)] + [(30, 1), (31, 1)]
+PE_UNIT = (4, 3)
+PE_TOK = P - S
+SC_UNIT = (7, 1)
+LAG = 2
+SC_PLAN = [0, 3, 5, 1, 1, 1, 1, 1, 1, 1, 1]
+PE_PLAN = [0, 0, 0, 2, 2, 2, 2, 2, 2]
+QUANTS = [(8, "pe", 0, 8 * P), (10, "pe", 8 * P, 4 * P), (12, "sc", 0, 4 * P)]
+MMS = [(11, "pe", 0), (12, "pe", 1), (13, "pe", 2), (14, "sc", 0)]
 
 FLOPS = 2 * S * N_TOK * H * R
 
@@ -32,18 +35,19 @@ FLOPS = 2 * S * N_TOK * H * R
 def tile_moe_pa_kernel(tc, encodings, domain_encs, Us, out):
     nc = tc.nc
     nu = len(UNITS)
-    sc = nu
     unit = dict(enumerate(UNITS))
-    unit[sc] = SC_UNIT
-    assert sum([c for (j, c) in UNITS]) + SC_UNIT[1] == NT and sum(LOADS) == NT
+    unit["pe"] = PE_UNIT
+    unit["sc"] = SC_UNIT
+    assert sum([c for (j, c) in UNITS + [PE_UNIT, SC_UNIT]]) == NT and sum(LOADS) == NT
 
     with ExitStack() as ctx:
         keep = ctx.enter_context(tc.tile_pool(name="keep", bufs=1))
         work = ctx.enter_context(tc.tile_pool(name="work", bufs=3))
         mxp = ctx.enter_context(tc.tile_pool(name="mxp", bufs=4))
-        ps_t = ctx.enter_context(tc.psum_pool(name="ps_t", bufs=3))
+        ps_t = ctx.enter_context(tc.psum_pool(name="ps_t", bufs=2))
         ps_s = ctx.enter_context(tc.psum_pool(name="ps_s", bufs=1))
-        ps_m = ctx.enter_context(tc.psum_pool(name="ps_m", bufs=4))
+        ps_x = ctx.enter_context(tc.psum_pool(name="ps_x", bufs=2))
+        ps_m = ctx.enter_context(tc.psum_pool(name="ps_m", bufs=3))
         ctx.enter_context(tc.manual_schedule())
 
         domq = keep.tile([P, S, 4], BF16)
@@ -54,6 +58,16 @@ def tile_moe_pa_kernel(tc, encodings, domain_encs, Us, out):
         nc.scalar.activation(out=warm[:], in_=one[:], func=ACT.Sqrt)
         ident = keep.tile([P, P], F32)
         make_identity(nc, ident[:])
+        sel = keep.tile([P, S, P], BF16)
+        for s in range(S):
+            nc.gpsimd.tensor_scalar(
+                out=sel[:, s, :],
+                in0=ident[:],
+                scalar1=1.0,
+                scalar2=ident[:, PE_TOK + s : PE_TOK + s + 1],
+                op0=ALU.mult,
+                op1=ALU.subtract,
+            )
 
         x_all = keep.tile([P, NT, H], BF16)
         enc_v = encodings.rearrange("(p j) h -> p j h", j=NT)
@@ -74,41 +88,49 @@ def tile_moe_pa_kernel(tc, encodings, domain_encs, Us, out):
             out=domrep[:].rearrange("p s (r t) -> p s r t", t=4),
             in_=domq[:].unsqueeze(2).to_broadcast([P, S, REP, 4]),
         )
+
         negdom = keep.tile([P, S, 4], F32)
+        nc.vector.tensor_scalar(out=negdom[:], in0=domq[:], scalar1=-1.0, scalar2=None, op0=ALU.mult)
 
         ugr = keep.tile([P, S * R * 4], BF16, align_bytes=64)
         ucodes = keep.tile([P, S * R], U32, align_bytes=64)
         uscl = keep.tile([P, S * R], U8, align_bytes=64)
         d2 = keep.tile([P, S, NT], F32)
-        dt_sc = keep.tile([P, S, SC_UNIT[1] * P * 4], BF16, align_bytes=64)
 
         tps = {}
-        dts = {sc: dt_sc}
+        dts = {}
         cds = {}
         scs = {}
+        for b in ("pe", "sc"):
+            n = S * unit[b][1] * P
+            dts[b] = keep.tile([P, S, unit[b][1] * P * 4], BF16, align_bytes=64, name="dt_" + b)
+            cds[b] = keep.tile([P, n], U32, align_bytes=64, name="cd_" + b)
+            scs[b] = keep.tile([P, n], U8, align_bytes=64, name="sl_" + b)
         w = REP * 4
 
         def stage_t(b):
             first, c = unit[b]
-            if b == sc:
+            if b == "sc":
                 tp = ps_s.tile([P, c * P, 2], F32, tag="ts")
             else:
-                tp = ps_t.tile([P, c * P, 2], F32, tag="tp")
+                tp = ps_t.tile([P, 2 * P, 2], F32, tag="tp")
             for i in range(c):
                 xw = x_all[:, first + i, :].bitcast(F32)
                 for u in range(2):
                     nc.tensor.transpose(tp[:, i * P : (i + 1) * P, u], xw[:, u : 2 * P : 2], ident[:])
             tps[b] = tp
 
-        def stage_d(b):
+        def stage_d(b, s0=0, s1=S):
             c = unit[b][1]
             gs = GS if c == 2 else 0
             nv = c * P - gs
-            dt = work.tile([P, S, c * P * 4], BF16, tag="dt", align_bytes=64)
+            if s0 == 0:
+                dts[b] = work.tile([P, S, c * P * 4], BF16, tag="dt", align_bytes=64, name="dt")
+            dt = dts[b]
             bank = tps[b][:].rearrange("p n u -> p (n u)")
             if gs:
                 eg = work.tile([P, gs * 4], BF16, tag="eg")
-                nc.vector.tensor_copy(out=eg[:].bitcast(F32), in_=bank[:, nv * 2 :])
+                nc.vector.tensor_copy(out=eg[:].bitcast(F32), in_=bank[:, nv * 2 : c * P * 2])
                 nc.gpsimd.tensor_tensor(
                     out=dt[:, :, nv * 4 :].rearrange("p s (g w) -> p s g w", w=w),
                     in0=eg[:].rearrange("p (g w) -> p g w", w=w).unsqueeze(1).to_broadcast([P, S, gs // REP, w]),
@@ -116,72 +138,121 @@ def tile_moe_pa_kernel(tc, encodings, domain_encs, Us, out):
                     op=ALU.subtract,
                 )
             nc.vector.tensor_tensor(
-                out=dt[:, :, 0 : nv * 4].rearrange("p s (g w) -> p s g w", w=w),
+                out=dt[:, s0:s1, 0 : nv * 4].rearrange("p s (g w) -> p s g w", w=w),
                 in0=bank[:, 0 : nv * 2]
                 .bitcast(BF16)
                 .rearrange("p (g w) -> p g w", w=w)
                 .unsqueeze(1)
-                .to_broadcast([P, S, nv // REP, w]),
-                in1=domrep[:].unsqueeze(2).to_broadcast([P, S, nv // REP, w]),
+                .to_broadcast([P, s1 - s0, nv // REP, w]),
+                in1=domrep[:, s0:s1, :].unsqueeze(2).to_broadcast([P, s1 - s0, nv // REP, w]),
                 op=ALU.subtract,
             )
-            dts[b] = dt
 
-        def sc_piece(i):
-            s, t = divmod(i, 4)
+        def sc_piece(q):
+            s, t = divmod(q, 4)
             nc.scalar.activation(
-                out=dt_sc[:, s, :].rearrange("p (n t) -> p n t", t=4)[:, :, t],
-                in_=tps[sc][:].rearrange("p n u -> p (n u)").bitcast(BF16).rearrange("p (n t) -> p n t", t=4)[:, :, t],
+                out=dts["sc"][:, s, :].rearrange("p (n t) -> p n t", t=4)[:, :, t],
+                in_=tps["sc"][:].rearrange("p n u -> p (n u)").bitcast(BF16).rearrange("p (n t) -> p n t", t=4)[:, :, t],
                 func=ACT.Identity,
                 bias=negdom[:, s, t : t + 1],
                 scale=1.0,
+            )
+
+        def pe_orphans():
+            first, c = PE_UNIT
+            tp = ps_x.tile([P, 2 * P, 2], F32, tag="px")
+            for i in reversed(range(c)):
+                xw = x_all[:, first + i, :].bitcast(F32)
+                for u in range(2):
+                    nc.tensor.transpose(tp[:, i * S : i * S + P, u], xw[:, u : 2 * P : 2], ident[:])
+            return tp
+
+        def pe_rows():
+            first, c = PE_UNIT
+            nc.scalar.dma_start(
+                out=x_all[PE_TOK:P, first : first + c, :],
+                in_=domain_encs.unsqueeze(1).to_broadcast([S, c, H]),
+            )
+
+        def pe_orphans_d(tp):
+            c = PE_UNIT[1]
+            n = S * 4
+            nc.vector.tensor_tensor(
+                out=dts["pe"][:].rearrange("p s (i w) -> p s i w", i=c)[:, :, :, PE_TOK * 4 :],
+                in0=tp[:].rearrange("p n u -> p (n u)")[:, PE_TOK * 2 : (PE_TOK + c * S) * 2]
+                .bitcast(BF16)
+                .rearrange("p (i w) -> p i w", w=n)
+                .unsqueeze(1)
+                .to_broadcast([P, S, c, n]),
+                in1=domrep[:, :, 0:n].unsqueeze(2).to_broadcast([P, S, c, n]),
+                op=ALU.subtract,
+            )
+
+        def pe_mm(q):
+            s, i = divmod(q, PE_UNIT[1])
+            px = ps_x.tile([P, 4, P], F32, tag="px")
+            for t in range(4):
+                nc.tensor.matmul(
+                    px[:, t, 0:PE_TOK],
+                    lhsT=x_all[:, PE_UNIT[0] + i, t:H:4],
+                    rhs=sel[:, s, 0:PE_TOK],
+                    start=True,
+                    stop=True,
+                )
+            return px
+
+        def pe_copy(q, px):
+            s, i = divmod(q, PE_UNIT[1])
+            lo = i * P * 4
+            nc.scalar.copy(
+                out=dts["pe"][:, s, lo : lo + PE_TOK * 4].rearrange("p (n t) -> p n t", t=4),
+                in_=px[:, :, 0:PE_TOK].rearrange("p t n -> p n t"),
+            )
+
+        def quant(b, lo, n):
+            nc.vector.quantize_mx(
+                out=cds[b][:, lo : lo + n].bitcast(FP8X4),
+                scales=scs[b][:, lo : lo + n],
+                in_=dts[b][:].rearrange("p s w -> p (s w)")[:, lo * 4 : (lo + n) * 4],
             )
 
         def stage_q(b):
             c = unit[b][1]
             cd = mxp.tile([P, S * c * P], U32, tag="cd", align_bytes=64)
             sl = mxp.tile([P, S * c * P], U8, tag="sl", align_bytes=64)
+            cds[b] = cd
+            scs[b] = sl
             parts = 2 if b == nu - 1 else 1
             n = S * c * P // parts
             for h in range(parts):
-                nc.vector.quantize_mx(
-                    out=cd[:, h * n : (h + 1) * n].bitcast(FP8X4),
-                    scales=sl[:, h * n : (h + 1) * n],
-                    in_=dts[b][:].rearrange("p s w -> p (s w)")[:, h * n * 4 : (h + 1) * n * 4],
-                )
-            cds[b] = cd
-            scs[b] = sl
+                quant(b, h * n, n)
 
-        def stage_m(b):
+        def tile_m(b, i):
             c = unit[b][1]
-            pjs = []
-            for i in range(c):
-                pj = ps_m.tile([P, S * R], F32, tag="pj")
-                for s in range(S):
-                    col = (s * c + i) * P
-                    nc.tensor.matmul_mx(
-                        out=pj[:, s * R : (s + 1) * R],
-                        lhsT=cds[b][:, col : col + P].bitcast(FP8X4),
-                        lhsT_scale=scs[b][:, col : col + P],
-                        rhs=ucodes[:, s * R : (s + 1) * R].bitcast(FP8X4),
-                        rhs_scale=uscl[:, s * R : (s + 1) * R],
-                        start=True,
-                        stop=True,
-                    )
-                pjs.append(pj)
-            return pjs
+            pj = ps_m.tile([P, S * R], F32, tag="pj")
+            for s in range(S):
+                col = (s * c + i) * P
+                nc.tensor.matmul_mx(
+                    out=pj[:, s * R : (s + 1) * R],
+                    lhsT=cds[b][:, col : col + P].bitcast(FP8X4),
+                    lhsT_scale=scs[b][:, col : col + P],
+                    rhs=ucodes[:, s * R : (s + 1) * R].bitcast(FP8X4),
+                    rhs_scale=uscl[:, s * R : (s + 1) * R],
+                    start=True,
+                    stop=True,
+                )
+            return pj
 
-        def stage_s(b, pjs):
-            for i, pj in enumerate(pjs):
-                j = unit[b][0] + i
-                for s in range(S):
-                    junk = work.tile([P, R], BF16, tag="junk")
-                    nc.scalar.activation(
-                        out=junk[:],
-                        in_=pj[:, s * R : (s + 1) * R],
-                        func=ACT.Square,
-                        accum_out=d2[:, s, j : j + 1],
-                    )
+        def tile_s(b, i, pj):
+            j = unit[b][0] + i
+            for s in range(S):
+                junk = work.tile([P, R], BF16, tag="junk")
+                nc.scalar.activation(
+                    out=junk[:],
+                    in_=pj[:, s * R : (s + 1) * R],
+                    func=ACT.Square,
+                    accum_out=d2[:, s, j : j + 1],
+                )
 
         def u_regroup(s):
             nc.scalar.copy(
@@ -189,35 +260,60 @@ def tile_moe_pa_kernel(tc, encodings, domain_encs, Us, out):
                 in_=uraw[:, s * R * 4 : (s + 1) * R * 4].rearrange("p (t r) -> p r t", t=4),
             )
 
+        sc_q = list(range(4 * S))
+        pe_q = list(range(S * PE_UNIT[1]))
+
+        stage_t(0)
         for k in range(nu + LAG):
-            if k < nu:
-                stage_t(k)
-            if k == SC_FIRST - 1:
-                stage_t(sc)
-            done = []
+            if k + 1 < nu:
+                stage_t(k + 1)
+            if k == 1:
+                orph = pe_orphans()
+                stage_t("sc")
+            tiles = []
             if k >= LAG:
-                done.append((k - LAG, stage_m(k - LAG)))
-            if k == SC_QUANT + LAG:
-                done.append((sc, stage_m(sc)))
-            if k == 1 or k == 2:
-                u_regroup(2 * k - 2)
-                u_regroup(2 * k - 1)
-            if k < nu:
-                stage_d(k)
-            if k == 2:
-                nc.vector.quantize_mx(out=ucodes[:].bitcast(FP8X4), scales=uscl[:], in_=ugr[:])
-                nc.vector.tensor_scalar(
-                    out=negdom[:], in0=domq[:], scalar1=-1.0, scalar2=None, op0=ALU.mult
-                )
-            if 1 <= k <= nu:
+                tiles = [(k - LAG, i) for i in range(unit[k - LAG][1])]
+            tiles = tiles + [(b, i) for (step, b, i) in MMS if step == k]
+            n_pe = PE_PLAN[k] if k < len(PE_PLAN) else 0
+            n = SC_PLAN[k] if k < len(SC_PLAN) else 0
+            now = sc_q[:n]
+            sc_q = sc_q[n:]
+            if k == 1:
+                for s in range(S):
+                    u_regroup(s)
+                pe_rows()
+            if k == nu - 1:
+                stage_d(k, 0, 2)
                 stage_q(k - 1)
-            if k == SC_QUANT:
-                stage_q(sc)
-            for i in range(SC_PER_STEP * (k - SC_FIRST), SC_PER_STEP * (k - SC_FIRST + 1)):
-                if 0 <= i < 4 * S:
-                    sc_piece(i)
-            for b, pjs in done:
-                stage_s(b, pjs)
+                stage_d(k, 2, S)
+            else:
+                if k < nu:
+                    stage_d(k)
+                if k == 2:
+                    nc.vector.quantize_mx(out=ucodes[:].bitcast(FP8X4), scales=uscl[:], in_=ugr[:])
+                if 1 <= k <= nu:
+                    stage_q(k - 1)
+            if k == 2:
+                pe_orphans_d(orph)
+            for step, b, lo, n in QUANTS:
+                if step == k:
+                    quant(b, lo, n)
+            pjs = [(b, i, tile_m(b, i)) for (b, i) in tiles]
+            pxs = [(q, pe_mm(q)) for q in pe_q[:n_pe]]
+            pe_q = pe_q[n_pe:]
+            while pxs or pjs or now:
+                if pjs:
+                    b, i, pj = pjs[0]
+                    tile_s(b, i, pj)
+                    pjs = pjs[1:]
+                if pxs:
+                    q, px = pxs[0]
+                    pe_copy(q, px)
+                    pxs = pxs[1:]
+                for q in now[:1]:
+                    sc_piece(q)
+                now = now[1:]
+        assert not sc_q and not pe_q
 
         dist = keep.tile([P, S, NT], F32)
         nc.scalar.activation(out=dist[:], in_=d2[:], func=ACT.Sqrt, bias=1e-30)

@@ -26,8 +26,8 @@ SC_UNIT = (7, 1)
 LAG = 2
 SC_PLAN = [0, 3, 5, 1, 1, 1, 1, 1, 1, 1, 1]
 PE_PLAN = [0, 0, 0, 2, 2, 2, 2, 2, 2]
-QUANTS = [(8, "pe", 0, 8 * P), (10, "pe", 8 * P, 4 * P), (12, "sc", 0, 4 * P)]
-MMS = [(11, "pe", 0), (12, "pe", 1), (13, "pe", 2), (14, "sc", 0)]
+QUANTS = [(8, "pe", 0, 8 * P), (9, "pe", 8 * P, 4 * P), (11, "sc", 0, 4 * P)]
+MMS = [(11, "pe", 0), (12, "pe", 1), (12, "pe", 2), (13, "sc", 0)]
 
 FLOPS = 2 * S * N_TOK * H * R
 
@@ -43,6 +43,7 @@ def tile_moe_pa_kernel(tc, encodings, domain_encs, Us, out):
     with ExitStack() as ctx:
         keep = ctx.enter_context(tc.tile_pool(name="keep", bufs=1))
         work = ctx.enter_context(tc.tile_pool(name="work", bufs=3))
+        diff = ctx.enter_context(tc.tile_pool(name="diff", bufs=3))
         mxp = ctx.enter_context(tc.tile_pool(name="mxp", bufs=4))
         ps_t = ctx.enter_context(tc.psum_pool(name="ps_t", bufs=2))
         ps_s = ctx.enter_context(tc.psum_pool(name="ps_s", bufs=1))
@@ -125,10 +126,10 @@ def tile_moe_pa_kernel(tc, encodings, domain_encs, Us, out):
             gs = GS if c == 2 else 0
             nv = c * P - gs
             if s0 == 0:
-                dts[b] = work.tile([P, S, c * P * 4], BF16, tag="dt", align_bytes=64, name="dt")
+                dts[b] = diff.tile([P, S, c * P * 4], BF16, tag="dt", align_bytes=64, name="dt")
             dt = dts[b]
             bank = tps[b][:].rearrange("p n u -> p (n u)")
-            if gs:
+            if gs and s0 == 0:
                 eg = work.tile([P, gs * 4], BF16, tag="eg")
                 nc.vector.tensor_copy(out=eg[:].bitcast(F32), in_=bank[:, nv * 2 : c * P * 2])
                 nc.gpsimd.tensor_tensor(
@@ -227,32 +228,35 @@ def tile_moe_pa_kernel(tc, encodings, domain_encs, Us, out):
             for h in range(parts):
                 quant(b, h * n, n)
 
-        def tile_m(b, i):
+        def unit_m(b, tiles):
             c = unit[b][1]
-            pj = ps_m.tile([P, S * R], F32, tag="pj")
-            for s in range(S):
-                col = (s * c + i) * P
-                nc.tensor.matmul_mx(
-                    out=pj[:, s * R : (s + 1) * R],
-                    lhsT=cds[b][:, col : col + P].bitcast(FP8X4),
-                    lhsT_scale=scs[b][:, col : col + P],
-                    rhs=ucodes[:, s * R : (s + 1) * R].bitcast(FP8X4),
-                    rhs_scale=uscl[:, s * R : (s + 1) * R],
-                    start=True,
-                    stop=True,
-                )
-            return pj
+            done = []
+            for i in tiles:
+                for s in range(S):
+                    if s == 0 or (s == 2 and b == nu - 1):
+                        pj = ps_m.tile([P, S * R], F32, tag="pj")
+                    col = (s * c + i) * P
+                    nc.tensor.matmul_mx(
+                        out=pj[:, s * R : (s + 1) * R],
+                        lhsT=cds[b][:, col : col + P].bitcast(FP8X4),
+                        lhsT_scale=scs[b][:, col : col + P],
+                        rhs=ucodes[:, s * R : (s + 1) * R].bitcast(FP8X4),
+                        rhs_scale=uscl[:, s * R : (s + 1) * R],
+                        start=True,
+                        stop=True,
+                    )
+                    done.append((b, i, s, pj))
+            return done
 
-        def tile_s(b, i, pj):
+        def square(b, i, s, pj):
             j = unit[b][0] + i
-            for s in range(S):
-                junk = work.tile([P, R], BF16, tag="junk")
-                nc.scalar.activation(
-                    out=junk[:],
-                    in_=pj[:, s * R : (s + 1) * R],
-                    func=ACT.Square,
-                    accum_out=d2[:, s, j : j + 1],
-                )
+            junk = work.tile([P, R], BF16, tag="junk")
+            nc.scalar.activation(
+                out=junk[:],
+                in_=pj[:, s * R : (s + 1) * R],
+                func=ACT.Square,
+                accum_out=d2[:, s, j : j + 1],
+            )
 
         def u_regroup(s):
             nc.scalar.copy(
@@ -265,24 +269,7 @@ def tile_moe_pa_kernel(tc, encodings, domain_encs, Us, out):
 
         stage_t(0)
         for k in range(nu + LAG):
-            if k + 1 < nu:
-                stage_t(k + 1)
-            if k == 1:
-                orph = pe_orphans()
-                stage_t("sc")
-            tiles = []
-            if k >= LAG:
-                tiles = [(k - LAG, i) for i in range(unit[k - LAG][1])]
-            tiles = tiles + [(b, i) for (step, b, i) in MMS if step == k]
-            n_pe = PE_PLAN[k] if k < len(PE_PLAN) else 0
-            n = SC_PLAN[k] if k < len(SC_PLAN) else 0
-            now = sc_q[:n]
-            sc_q = sc_q[n:]
-            if k == 1:
-                for s in range(S):
-                    u_regroup(s)
-                pe_rows()
-            if k == nu - 1:
+            if nu - 2 <= k < nu:
                 stage_d(k, 0, 2)
                 stage_q(k - 1)
                 stage_d(k, 2, S)
@@ -298,14 +285,31 @@ def tile_moe_pa_kernel(tc, encodings, domain_encs, Us, out):
             for step, b, lo, n in QUANTS:
                 if step == k:
                     quant(b, lo, n)
-            pjs = [(b, i, tile_m(b, i)) for (b, i) in tiles]
+            if k + 1 < nu - 2:
+                stage_t(k + 1)
+            squares = []
+            if k >= LAG:
+                squares = unit_m(k - LAG, list(range(unit[k - LAG][1])))
+            if nu - 2 <= k + 1 < nu:
+                stage_t(k + 1)
+            if k == 1:
+                orph = pe_orphans()
+                stage_t("sc")
+            n_pe = PE_PLAN[k] if k < len(PE_PLAN) else 0
             pxs = [(q, pe_mm(q)) for q in pe_q[:n_pe]]
             pe_q = pe_q[n_pe:]
-            while pxs or pjs or now:
-                if pjs:
-                    b, i, pj = pjs[0]
-                    tile_s(b, i, pj)
-                    pjs = pjs[1:]
+            n_sc = SC_PLAN[k] if k < len(SC_PLAN) else 0
+            now = sc_q[:n_sc]
+            sc_q = sc_q[n_sc:]
+            if k == 1:
+                for s in range(S):
+                    u_regroup(s)
+            if k == 1:
+                pe_rows()
+            while squares or pxs or now:
+                for sq in squares[:4]:
+                    square(*sq)
+                squares = squares[4:]
                 if pxs:
                     q, px = pxs[0]
                     pe_copy(q, px)
@@ -313,6 +317,10 @@ def tile_moe_pa_kernel(tc, encodings, domain_encs, Us, out):
                 for q in now[:1]:
                     sc_piece(q)
                 now = now[1:]
+            for step, b, i in MMS:
+                if step == k:
+                    for sq in unit_m(b, [i]):
+                        square(*sq)
         assert not sc_q and not pe_q
 
         dist = keep.tile([P, S, NT], F32)

@@ -59,15 +59,12 @@ def tile_moe_pa_kernel(tc, encodings, domain_encs, Us, out):
         nc.scalar.activation(out=warm[:], in_=one[:], func=ACT.Sqrt)
         ident = keep.tile([P, P], F32)
         make_identity(nc, ident[:])
+        ncol = keep.tile([P, S], F32)
+        nc.scalar.activation(out=ncol[:], in_=ident[:, PE_TOK:], func=ACT.Copy, scale=-1.0)
         sel = keep.tile([P, S, P], BF16)
         for s in range(S):
-            nc.gpsimd.tensor_scalar(
-                out=sel[:, s, :],
-                in0=ident[:],
-                scalar1=1.0,
-                scalar2=ident[:, PE_TOK + s : PE_TOK + s + 1],
-                op0=ALU.mult,
-                op1=ALU.subtract,
+            nc.scalar.activation(
+                out=sel[:, s, :], in_=ident[:], func=ACT.Identity, bias=ncol[:, s : s + 1], scale=1.0
             )
 
         x_all = keep.tile([P, NT, H], BF16)

from contextlib import ExitStack

import concourse.mybir as mybir
from concourse.masks import make_identity

F32 = mybir.dt.float32
BF16 = mybir.dt.bfloat16
U32 = mybir.dt.uint32
U8 = mybir.dt.uint8
FP8X4 = mybir.dt.float8_e4m3fn_x4
ALU = mybir.AluOpType
ACT = mybir.ActivationFunctionType
AX = mybir.AxisListType

P = 128
N_TOK, H, S, R = 4096, 512, 4, 128
NT = N_TOK // P
REP = 8
GS = 40
LOADS = [1, 1, 2, 4, 8, 16]
U_AFTER = 2
UNITS = [(0, 1), (1, 1), (2, 2)] + [(j, 2) for j in range(8, 30, 2)] + [(30, 1), (31, 1)]
PE_UNIT = (4, 3)
PE_TOK = P - S
SC_UNIT = (7, 1)
LAG = 2
SC_PLAN = [0, 3, 5, 1, 1, 1, 1, 1, 1, 1, 1]
PE_PLAN = [0, 0, 0, 2, 2, 2, 2, 2, 2]
QUANTS = [(8, "pe", 0, 8 * P), (9, "pe", 8 * P, 4 * P), (11, "sc", 0, 4 * P)]
MMS = [(11, "pe", 0), (12, "pe", 1), (12, "pe", 2), (13, "sc", 0)]

FLOPS = 2 * S * N_TOK * H * R


def tile_moe_pa_kernel(tc, encodings, domain_encs, Us, out):
    nc = tc.nc
    nu = len(UNITS)
    unit = dict(enumerate(UNITS))
    unit["pe"] = PE_UNIT
    unit["sc"] = SC_UNIT
    assert sum([c for (j, c) in UNITS + [PE_UNIT, SC_UNIT]]) == NT and sum(LOADS) == NT

    with ExitStack() as ctx:
        keep = ctx.enter_context(tc.tile_pool(name="keep", bufs=1))
        work = ctx.enter_context(tc.tile_pool(name="work", bufs=3))
        diff = ctx.enter_context(tc.tile_pool(name="diff", bufs=3))
        mxp = ctx.enter_context(tc.tile_pool(name="mxp", bufs=4))
        ps_t = ctx.enter_context(tc.psum_pool(name="ps_t", bufs=2))
        ps_s = ctx.enter_context(tc.psum_pool(name="ps_s", bufs=1))
        ps_x = ctx.enter_context(tc.psum_pool(name="ps_x", bufs=2))
        ps_m = ctx.enter_context(tc.psum_pool(name="ps_m", bufs=3))
        ctx.enter_context(tc.manual_schedule())

        domq = keep.tile([P, S, 4], BF16)
        nc.scalar.dma_start(out=domq[:], in_=domain_encs.rearrange("s (p t) -> p s t", t=4))
        one = keep.tile([P, 1], F32)
        nc.vector.memset(one[:], 1.0)
        warm = keep.tile([P, 1], F32)
        nc.scalar.activation(out=warm[:], in_=one[:], func=ACT.Sqrt)
        ident = keep.tile([P, P], F32)
        make_identity(nc, ident[:])
        ncol = keep.tile([P, S], F32)
        nc.scalar.activation(out=ncol[:], in_=ident[:, PE_TOK:], func=ACT.Copy, scale=-1.0)
        sel = keep.tile([P, S, P], BF16)
        for s in range(S):
            nc.scalar.activation(
                out=sel[:, s, :], in_=ident[:], func=ACT.Identity, bias=ncol[:, s : s + 1], scale=1.0
            )

        x_all = keep.tile([P, NT, H], BF16)
        enc_v = encodings.rearrange("(p j) h -> p j h", j=NT)
        uraw = keep.tile([P, S * 4 * R], BF16)

        j0 = 0
        for i, cnt in enumerate(LOADS):
            if i == U_AFTER:
                nc.sync.dma_start(
                    out=uraw[:].rearrange("p (s w) -> p s w", w=4 * R),
                    in_=Us.rearrange("s (p t) r -> p s (t r)", t=4),
                )
            nc.sync.dma_start(out=x_all[:, j0 : j0 + cnt, :], in_=enc_v[:, j0 : j0 + cnt, :])
            j0 += cnt

        domrep = keep.tile([P, S, REP * 4], BF16)
        nc.vector.tensor_copy(
            out=domrep[:].rearrange("p s (r t) -> p s r t", t=4),
            in_=domq[:].unsqueeze(2).to_broadcast([P, S, REP, 4]),
        )

        negdom = keep.tile([P, S, 4], F32)
        nc.vector.tensor_scalar(out=negdom[:], in0=domq[:], scalar1=-1.0, scalar2=None, op0=ALU.mult)

        ugr = keep.tile([P, S * R * 4], BF16, align_bytes=64)
        ucodes = keep.tile([P, S * R], U32, align_bytes=64)
        uscl = keep.tile([P, S * R], U8, align_bytes=64)
        d2 = keep.tile([P, S, NT], F32)

        tps = {}
        dts = {}
        cds = {}
        scs = {}
        for b in ("pe", "sc"):
            n = S * unit[b][1] * P
            dts[b] = keep.tile([P, S, unit[b][1] * P * 4], BF16, align_bytes=64, name="dt_" + b)
            cds[b] = keep.tile([P, n], U32, align_bytes=64, name="cd_" + b)
            scs[b] = keep.tile([P, n], U8, align_bytes=64, name="sl_" + b)
        w = REP * 4

        def stage_t(b):
            first, c = unit[b]
            if b == "sc":
                tp = ps_s.tile([P, c * P, 2], F32, tag="ts")
            else:
                tp = ps_t.tile([P, 2 * P, 2], F32, tag="tp")
            for i in range(c):
                xw = x_all[:, first + i, :].bitcast(F32)
                for u in range(2):
                    nc.tensor.transpose(tp[:, i * P : (i + 1) * P, u], xw[:, u : 2 * P : 2], ident[:])
            tps[b] = tp

        def stage_d(b, s0=0, s1=S):
            c = unit[b][1]
            gs = GS if c == 2 else 0
            nv = c * P - gs
            if s0 == 0:
                dts[b] = diff.tile([P, S, c * P * 4], BF16, tag="dt", align_bytes=64, name="dt")
            dt = dts[b]
            bank = tps[b][:].rearrange("p n u -> p (n u)")
            if gs and s0 == 0:
                eg = work.tile([P, gs * 4], BF16, tag="eg")
                nc.vector.tensor_copy(out=eg[:].bitcast(F32), in_=bank[:, nv * 2 : c * P * 2])
                nc.gpsimd.tensor_tensor(
                    out=dt[:, :, nv * 4 :].rearrange("p s (g w) -> p s g w", w=w),
                    in0=eg[:].rearrange("p (g w) -> p g w", w=w).unsqueeze(1).to_broadcast([P, S, gs // REP, w]),
                    in1=domrep[:].unsqueeze(2).to_broadcast([P, S, gs // REP, w]),
                    op=ALU.subtract,
                )
            nc.vector.tensor_tensor(
                out=dt[:, s0:s1, 0 : nv * 4].rearrange("p s (g w) -> p s g w", w=w),
                in0=bank[:, 0 : nv * 2]
                .bitcast(BF16)
                .rearrange("p (g w) -> p g w", w=w)
                .unsqueeze(1)
                .to_broadcast([P, s1 - s0, nv // REP, w]),
                in1=domrep[:, s0:s1, :].unsqueeze(2).to_broadcast([P, s1 - s0, nv // REP, w]),
                op=ALU.subtract,
            )

        def sc_piece(q):
            s, t = divmod(q, 4)
            nc.scalar.activation(
                out=dts["sc"][:, s, :].rearrange("p (n t) -> p n t", t=4)[:, :, t],
                in_=tps["sc"][:].rearrange("p n u -> p (n u)").bitcast(BF16).rearrange("p (n t) -> p n t", t=4)[:, :, t],
                func=ACT.Identity,
                bias=negdom[:, s, t : t + 1],
                scale=1.0,
            )

        def pe_orphans():
            first, c = PE_UNIT
            tp = ps_x.tile([P, 2 * P, 2], F32, tag="px")
            for i in reversed(range(c)):
                xw = x_all[:, first + i, :].bitcast(F32)
                for u in range(2):
                    nc.tensor.transpose(tp[:, i * S : i * S + P, u], xw[:, u : 2 * P : 2], ident[:])
            return tp

        def pe_rows():
            first, c = PE_UNIT
            nc.scalar.dma_start(
                out=x_all[PE_TOK:P, first : first + c, :],
                in_=domain_encs.unsqueeze(1).to_broadcast([S, c, H]),
            )

        def pe_orphans_d(tp):
            c = PE_UNIT[1]
            n = S * 4
            nc.vector.tensor_tensor(
                out=dts["pe"][:].rearrange("p s (i w) -> p s i w", i=c)[:, :, :, PE_TOK * 4 :],
                in0=tp[:].rearrange("p n u -> p (n u)")[:, PE_TOK * 2 : (PE_TOK + c * S) * 2]
                .bitcast(BF16)
                .rearrange("p (i w) -> p i w", w=n)
                .unsqueeze(1)
                .to_broadcast([P, S, c, n]),
                in1=domrep[:, :, 0:n].unsqueeze(2).to_broadcast([P, S, c, n]),
                op=ALU.subtract,
            )

        def pe_mm(q):
            s, i = divmod(q, PE_UNIT[1])
            px = ps_x.tile([P, 4, P], F32, tag="px")
            for t in range(4):
                nc.tensor.matmul(
                    px[:, t, 0:PE_TOK],
                    lhsT=x_all[:, PE_UNIT[0] + i, t:H:4],
                    rhs=sel[:, s, 0:PE_TOK],
                    start=True,
                    stop=True,
                )
            return px

        def pe_copy(q, px):
            s, i = divmod(q, PE_UNIT[1])
            lo = i * P * 4
            nc.scalar.copy(
                out=dts["pe"][:, s, lo : lo + PE_TOK * 4].rearrange("p (n t) -> p n t", t=4),
                in_=px[:, :, 0:PE_TOK].rearrange("p t n -> p n t"),
            )

        def quant(b, lo, n):
            nc.vector.quantize_mx(
                out=cds[b][:, lo : lo + n].bitcast(FP8X4),
                scales=scs[b][:, lo : lo + n],
                in_=dts[b][:].rearrange("p s w -> p (s w)")[:, lo * 4 : (lo + n) * 4],
            )

        def stage_q(b):
            c = unit[b][1]
            cd = mxp.tile([P, S * c * P], U32, tag="cd", align_bytes=64)
            sl = mxp.tile([P, S * c * P], U8, tag="sl", align_bytes=64)
            cds[b] = cd
            scs[b] = sl
            parts = 2 if b == nu - 1 else 1
            n = S * c * P // parts
            for h in range(parts):
                quant(b, h * n, n)

        def unit_m(b, tiles):
            c = unit[b][1]
            done = []
            for i in tiles:
                for s in range(S):
                    if s == 0 or (s == 2 and b == nu - 1):
                        pj = ps_m.tile([P, S * R], F32, tag="pj")
                    col = (s * c + i) * P
                    nc.tensor.matmul_mx(
                        out=pj[:, s * R : (s + 1) * R],
                        lhsT=cds[b][:, col : col + P].bitcast(FP8X4),
                        lhsT_scale=scs[b][:, col : col + P],
                        rhs=ucodes[:, s * R : (s + 1) * R].bitcast(FP8X4),
                        rhs_scale=uscl[:, s * R : (s + 1) * R],
                        start=True,
                        stop=True,
                    )
                    done.append((b, i, s, pj))
            return done

        def square(b, i, s, pj):
            j = unit[b][0] + i
            junk = work.tile([P, R], BF16, tag="junk")
            nc.scalar.activation(
                out=junk[:],
                in_=pj[:, s * R : (s + 1) * R],
                func=ACT.Square,
                accum_out=d2[:, s, j : j + 1],
            )

        def u_regroup(s):
            nc.scalar.copy(
                out=ugr[:, s * R * 4 : (s + 1) * R * 4].rearrange("p (r t) -> p r t", t=4),
                in_=uraw[:, s * R * 4 : (s + 1) * R * 4].rearrange("p (t r) -> p r t", t=4),
            )

        sc_q = list(range(4 * S))
        pe_q = list(range(S * PE_UNIT[1]))

        stage_t(0)
        for k in range(nu + LAG):
            if nu - 2 <= k < nu:
                stage_d(k, 0, 2)
                stage_q(k - 1)
                stage_d(k, 2, S)
            else:
                if k < nu:
                    stage_d(k)
                if k == 2:
                    nc.vector.quantize_mx(out=ucodes[:].bitcast(FP8X4), scales=uscl[:], in_=ugr[:])
                if 1 <= k <= nu:
                    stage_q(k - 1)
            if k == 2:
                pe_orphans_d(orph)
            for step, b, lo, n in QUANTS:
                if step == k:
                    quant(b, lo, n)
            if k + 1 < nu - 2:
                stage_t(k + 1)
            squares = []
            if k >= LAG:
                squares = unit_m(k - LAG, list(range(unit[k - LAG][1])))
            if nu - 2 <= k + 1 < nu:
                stage_t(k + 1)
            if k == 1:
                orph = pe_orphans()
                stage_t("sc")
            n_pe = PE_PLAN[k] if k < len(PE_PLAN) else 0
            pxs = [(q, pe_mm(q)) for q in pe_q[:n_pe]]
            pe_q = pe_q[n_pe:]
            n_sc = SC_PLAN[k] if k < len(SC_PLAN) else 0
            now = sc_q[:n_sc]
            sc_q = sc_q[n_sc:]
            if k == 1:
                for s in range(S):
                    u_regroup(s)
            if k == 1:
                pe_rows()
            while squares or pxs or now:
                for sq in squares[:4]:
                    square(*sq)
                squares = squares[4:]
                if pxs:
                    q, px = pxs[0]
                    pe_copy(q, px)
                    pxs = pxs[1:]
                for q in now[:1]:
                    sc_piece(q)
                now = now[1:]
            for step, b, i in MMS:
                if step == k:
                    for sq in unit_m(b, [i]):
                        square(*sq)
        assert not sc_q and not pe_q

        dist = keep.tile([P, S, NT], F32)
        nc.scalar.activation(out=dist[:], in_=d2[:], func=ACT.Sqrt, bias=1e-30)
        warm2 = keep.tile([P, 1], F32)
        nc.scalar.activation(out=warm2[:], in_=dist[:, 0, 0:1], func=ACT.Exp, scale=-1.0)
        dmin = keep.tile([P, NT], F32)
        nc.vector.tensor_reduce(out=dmin[:], in_=dist[:].rearrange("p s j -> p j s"), axis=AX.X, op=ALU.min)
        z = keep.tile([P, S, NT], F32)
        nc.vector.tensor_tensor(
            out=z[:], in0=dmin[:].unsqueeze(1).to_broadcast([P, S, NT]), in1=dist[:], op=ALU.subtract
        )
        e = keep.tile([P, S, NT], F32)
        nc.scalar.activation(out=e[:], in_=z[:], func=ACT.Exp)
        esum = keep.tile([P, NT], F32)
        nc.vector.tensor_reduce(out=esum[:], in_=e[:].rearrange("p s j -> p j s"), axis=AX.X, op=ALU.add)
        rsum = keep.tile([P, NT], F32)
        nc.vector.reciprocal(out=rsum[:], in_=esum[:])
        res = keep.tile([P, S, NT], F32)
        nc.vector.tensor_tensor(
            out=res[:], in0=e[:], in1=rsum[:].unsqueeze(1).to_broadcast([P, S, NT]), op=ALU.mult
        )
        nc.sync.dma_start(out=out.rearrange("s (p j) -> p s j", j=NT), in_=res[:])
